import numpy as np
import ml_dtypes


def mxq(x, axis, fmt="e4m3"):
    dtype, down = {"e4m3": (ml_dtypes.float8_e4m3fn, 7), "e5m2": (ml_dtypes.float8_e5m2, 14)}[fmt]
    v = np.moveaxis(np.asarray(x, np.float32).astype(ml_dtypes.bfloat16).astype(np.float64), axis, -1)
    blocks = v.reshape(v.shape[:-1] + (-1, 32))
    amax = np.abs(blocks).max(-1, keepdims=True)
    byte = np.maximum(np.where(amax > 0, np.frexp(amax)[1] - 1 + 127, 0) - down, 1)
    scale = np.exp2(byte - 127.0)
    codes = (blocks / scale).astype(np.float32).astype(dtype).astype(np.float64)
    return np.moveaxis((codes * scale).reshape(v.shape), -1, axis)


WIDE = False


def mx_kscale(k):
    if not WIDE:
        return np.ones(k)
    levels = np.array([10, -10, 5, -5, 0])
    a = np.random.permutation(np.resize(levels, k // 512 * 4)).reshape(k // 512, 4)
    idx = np.arange(k)
    return np.exp2(a[idx // 512, idx % 128 // 32])


BF16 = ml_dtypes.bfloat16


def bf(x):
    return np.asarray(x, np.float32).astype(BF16)


def f64(x):
    return np.asarray(x).astype(np.float64)


E2M1 = np.array([0.0, 0.5, 1.0, 1.5, 2.0, 3.0, 4.0, 6.0, -0.0, -0.5, -1.0, -1.5, -2.0, -3.0, -4.0, -6.0])


def pack_weight(w, fmt):
    k, n = w.shape
    w = f64(bf(w)).reshape(k // 32, 32, n)
    amax = np.abs(w).max(1)
    if fmt == "e4m3":
        byte = np.frexp(amax)[1] - 1 + 127 - 7
    else:
        mant, ex = np.frexp(amax / 6.0)
        byte = np.where(mant > 0.5, ex, ex - 1) + 127
    byte = np.clip(np.where(amax > 0, byte, 1), 1, 254)
    scaled = (w * np.exp2(127.0 - byte)[:, None, :]).reshape(k, n).astype(np.float32)
    by_word = np.ascontiguousarray(scaled.reshape(k // 512, 128, 4, n).transpose(0, 1, 3, 2))
    if fmt == "e4m3":
        words = by_word.astype(ml_dtypes.float8_e4m3fn).view(np.uint8)
    else:
        c = by_word.astype(ml_dtypes.float4_e2m1fn).view(np.uint8) & 0xF
        words = c[..., 0::2] | (c[..., 1::2] << 4)
    return np.ascontiguousarray(words), np.ascontiguousarray(byte.astype(np.uint8).reshape(k // 512, 16, n))


def unpack_weight(words, scales, fmt):
    g, p, n, _ = words.shape
    if fmt == "e4m3":
        vals = np.ascontiguousarray(words).view(ml_dtypes.float8_e4m3fn).astype(np.float64)
    else:
        nib = np.empty((g, p, n, 4), np.uint8)
        nib[..., 0::2] = words & 0xF
        nib[..., 1::2] = words >> 4
        vals = E2M1[nib]
    vals = vals * np.repeat(np.exp2(scales.astype(np.float64) - 127.0), 8, axis=1)[..., None]
    return vals.transpose(0, 1, 3, 2).reshape(g * 512, n)


B, S, T, E, D, H = 1, 128, 128, 16384, 2048, 16
DK = D // H


def rope_tables(n):
    m = np.arange(n, dtype=np.float64)[:, None]
    i = np.repeat(np.arange(DK // 2, dtype=np.float64), 2)[None, :]
    ang = m * np.exp(-(2.0 * np.log(1e4) / DK) * i)
    return np.cos(ang), np.sin(ang)


def rotate_pairs(x):
    return np.stack([-x[..., 1::2], x[..., 0::2]], axis=-1).reshape(x.shape)


def setup_inputs():
    s = mx_kscale(E)
    x = bf(np.random.standard_normal((B, S, E)) * s)
    w_words, w_scales = pack_weight(np.random.standard_normal((E, D)) * 1.1 / np.sqrt(E) / s[:, None], "e4m3")
    b = bf(np.random.standard_normal(D) * 0.4)
    return {"x": x, "w_words": w_words, "w_scales": w_scales, "b": b}


def reference(x, w_words, w_scales, b):
    p = (mxq(f64(x), 2, "e4m3") @ unpack_weight(w_words, w_scales, "e4m3")) + f64(b)
    p = p.reshape(B, S, H, DK).transpose(0, 2, 1, 3)
    r1, r2 = rope_tables(S)
    return p * r1 + rotate_pairs(p) * r2

@@ -1,0 +1,253 @@
+import math
+from contextlib import ExitStack
+
+import concourse.mybir as mybir
+from concourse.masks import make_identity
+
+F32 = mybir.dt.float32
+BF16 = mybir.dt.bfloat16
+I32 = mybir.dt.int32
+U32 = mybir.dt.uint32
+U8 = mybir.dt.uint8
+FP8X4 = mybir.dt.float8_e4m3fn_x4
+ALU = mybir.AluOpType
+ACT = mybir.ActivationFunctionType
+
+P = 128
+PACK = 4
+K_PASS = P * PACK
+TOKENS = 128
+K = 16384
+D = 2048
+HEADS = 16
+HEAD_DIM = 128
+PAIRS = HEAD_DIM // 2
+GROUPS = K // K_PASS
+BANK = 512
+BANKS = D // BANK
+HEADS_PER_BANK = BANK // HEAD_DIM
+
+X_LOADS = 4
+GROUPS_PER_LOAD = GROUPS // X_LOADS
+GROUPS_PER_BANK = 2
+
+PLANES_PER_TILE = 4
+PLANE_TILES = GROUPS // PLANES_PER_TILE
+
+WHOLE_GROUPS = GROUPS - BANKS
+W_STEPS = WHOLE_GROUPS + BANKS
+W_BYTES = D * PACK
+W_BUFS = 12
+W_AHEAD = W_BUFS - 1
+
+PI_HIGH = 3.140625
+PI_MIDDLE = int((math.pi - PI_HIGH) * 2.0**27) / 2.0**27
+PI_LOW = math.pi - PI_HIGH - PI_MIDDLE
+
+FLOPS = 2 * TOKENS * K * D
+
+
+def tile_multiheadedattention_pa_k_kernel(tc, x, w_words, w_scales, b, out):
+    nc = tc.nc
+    with ExitStack() as ctx:
+        ctx.enter_context(tc.manual_schedule())
+        keep = ctx.enter_context(tc.tile_pool(name="keep", bufs=1))
+        x_pool = ctx.enter_context(tc.tile_pool(name="x_pool", bufs=X_LOADS))
+        stage = ctx.enter_context(tc.tile_pool(name="stage", bufs=2))
+        w_pool = ctx.enter_context(tc.tile_pool(name="w_pool", bufs=W_BUFS))
+        acc_pool = ctx.enter_context(tc.psum_pool(name="acc_pool", bufs=1))
+        work_pool = ctx.enter_context(tc.psum_pool(name="work_pool", bufs=8 - BANKS))
+
+        identity = keep.tile([P, P], F32)
+        make_identity(nc, identity[:])
+        pair_index = keep.tile([P, PAIRS], I32)
+        nc.gpsimd.iota(pair_index[:], pattern=[[1, PAIRS]], base=0, channel_multiplier=0)
+        position = keep.tile([P, 1], I32)
+        nc.gpsimd.iota(position[:], pattern=[[0, 1]], base=0, channel_multiplier=1)
+
+        bias_row = keep.tile([P, D], BF16)
+        nc.vector.memset(bias_row[:], 0.0)
+        ones = keep.tile([P, P], BF16)
+        nc.vector.memset(ones[:], 1.0)
+        w_planes = keep.tile([P, PLANE_TILES, D], U8, align_bytes=64)
+        nc.vector.memset(w_planes[:].bitcast(I32), 0)
+
+        nc.scalar.dma_start(out=bias_row[0:1, :], in_=b.rearrange("(o n) -> o n", o=1))
+
+        x_cols = K // X_LOADS
+        x_raw = []
+        for load in range(X_LOADS):
+            x_tile = x_pool.tile([P, x_cols], BF16, name="x_tile")
+            nc.sync.dma_start(out=x_tile[:], in_=x[0, :, load * x_cols : (load + 1) * x_cols])
+            x_raw.append(x_tile)
+
+        for j in range(PLANE_TILES):
+            for quadrant in (0, 2, 1, 3):
+                nc.sync.dma_start(
+                    out=w_planes[32 * quadrant : 32 * quadrant + 16, j, :].bitcast(I32),
+                    in_=w_scales[
+                        PLANES_PER_TILE * j : PLANES_PER_TILE * (j + 1),
+                        4 * quadrant : 4 * quadrant + 4,
+                        :,
+                    ].bitcast(I32),
+                )
+
+        def load_weights(step):
+            w_tile = w_pool.tile([P, W_BYTES], U8, name="w_tile", align_bytes=64)
+            if step < WHOLE_GROUPS:
+                nc.sync.dma_start(
+                    out=w_tile[:].bitcast(I32),
+                    in_=w_words[step].rearrange("p n t -> p (n t)").bitcast(I32),
+                )
+            else:
+                bank = step - WHOLE_GROUPS
+                nc.sync.dma_start(
+                    out=w_tile[:].rearrange("p (g c) -> p g c", g=BANKS).bitcast(I32),
+                    in_=w_words[WHOLE_GROUPS:, :, bank * BANK : (bank + 1) * BANK, :]
+                    .rearrange("g p n t -> p g (n t)")
+                    .bitcast(I32),
+                )
+            return w_tile
+
+        w_tiles = [load_weights(step) for step in range(W_AHEAD)]
+
+        x_codes = keep.tile([P, GROUPS * TOKENS], U32, align_bytes=64)
+        x_scales = keep.tile([P, GROUPS * TOKENS], U8, align_bytes=64)
+        for load in range(X_LOADS):
+            x_words = x_raw[load][:].bitcast(F32)
+            grouped = stage.tile([P, GROUPS_PER_LOAD, TOKENS, PACK], BF16, align_bytes=64)
+            for bank in range(GROUPS_PER_LOAD // GROUPS_PER_BANK):
+                turned = work_pool.tile([P, GROUPS_PER_BANK, 2, TOKENS], F32, name="work")
+                for local in range(GROUPS_PER_BANK):
+                    first = (K_PASS // 2) * (bank * GROUPS_PER_BANK + local)
+                    for u in range(2):
+                        nc.tensor.transpose(
+                            turned[:, local, u, :],
+                            x_words[:, first + u : first + K_PASS // 2 : 2],
+                            identity[:],
+                        )
+                groups = slice(bank * GROUPS_PER_BANK, (bank + 1) * GROUPS_PER_BANK)
+                side_by_side = grouped[:, groups, :, :].bitcast(F32)
+                if bank % 2 == 0:
+                    nc.scalar.copy(out=side_by_side, in_=turned[:].rearrange("p g u m -> p g m u"))
+                else:
+                    nc.vector.tensor_copy(
+                        out=side_by_side, in_=turned[:].rearrange("p g u m -> p g m u")
+                    )
+            cols = slice(load * GROUPS_PER_LOAD * TOKENS, (load + 1) * GROUPS_PER_LOAD * TOKENS)
+            nc.vector.quantize_mx(
+                out=x_codes[:, cols].bitcast(FP8X4),
+                scales=x_scales[:, cols],
+                in_=grouped[:].rearrange("p g m t -> p (g m t)"),
+            )
+
+        bias_all = keep.tile([P, D], F32)
+        for bank in range(BANKS):
+            cols = slice(bank * BANK, (bank + 1) * BANK)
+            spread = work_pool.tile([P, BANK], F32, name="work")
+            nc.tensor.matmul(out=spread[:], lhsT=ones[:], rhs=bias_row[:, cols], start=True, stop=True)
+            nc.scalar.copy(out=bias_all[:, cols], in_=spread[:])
+
+        pair_f = keep.tile([P, PAIRS], F32)
+        nc.vector.tensor_copy(out=pair_f[:], in_=pair_index[:])
+        position_f = keep.tile([P, 1], F32)
+        nc.vector.tensor_copy(out=position_f[:], in_=position[:])
+        frequency = keep.tile([P, PAIRS], F32)
+        nc.scalar.activation(
+            out=frequency[:], in_=pair_f[:], func=ACT.Exp, scale=-2.0 * math.log(10000.0) / HEAD_DIM
+        )
+        angle = keep.tile([P, 2 * PAIRS], F32)
+        nc.vector.tensor_scalar(
+            out=angle[:, 0:PAIRS], in0=frequency[:], scalar1=position_f[:, 0:1],
+            scalar2=math.pi / 2.0, op0=ALU.mult, op1=ALU.add,
+        )
+        nc.vector.tensor_scalar(
+            out=angle[:, PAIRS:], in0=frequency[:], scalar1=position_f[:, 0:1],
+            scalar2=None, op0=ALU.mult,
+        )
+        half_turns_f = keep.tile([P, 2 * PAIRS], F32)
+        nc.vector.tensor_scalar(
+            out=half_turns_f[:], in0=angle[:], scalar1=1.0 / math.pi, scalar2=None, op0=ALU.mult
+        )
+        half_turns_i = keep.tile([P, 2 * PAIRS], I32)
+        nc.vector.tensor_copy(out=half_turns_i[:], in_=half_turns_f[:])
+        half_turns = keep.tile([P, 2 * PAIRS], F32)
+        nc.vector.tensor_copy(out=half_turns[:], in_=half_turns_i[:])
+        for part in (PI_HIGH, PI_MIDDLE, PI_LOW):
+            nc.vector.scalar_tensor_tensor(
+                out=angle[:], in0=half_turns[:], scalar=-part, in1=angle[:],
+                op0=ALU.mult, op1=ALU.add,
+            )
+        sine = keep.tile([P, 2 * PAIRS], F32)
+        nc.scalar.activation(out=sine[:], in_=angle[:], func=ACT.Sin)
+        odd = keep.tile([P, 2 * PAIRS], I32)
+        nc.vector.tensor_single_scalar(out=odd[:], in_=half_turns_i[:], scalar=1, op=ALU.bitwise_and)
+        sign = keep.tile([P, 2 * PAIRS], F32)
+        nc.vector.tensor_scalar(
+            out=sign[:], in0=odd[:], scalar1=-2.0, scalar2=1.0, op0=ALU.mult, op1=ALU.add
+        )
+        cos_sin = keep.tile([P, 2 * PAIRS], F32)
+        nc.vector.tensor_mul(out=cos_sin[:], in0=sine[:], in1=sign[:])
+        minus_sin = keep.tile([P, PAIRS], F32)
+        nc.vector.tensor_scalar(
+            out=minus_sin[:], in0=cos_sin[:, PAIRS:], scalar1=-1.0, scalar2=None, op0=ALU.mult
+        )
+        by_head = [P, HEADS_PER_BANK, PAIRS]
+        cos_pairs = cos_sin[:, 0:PAIRS].unsqueeze(1).unsqueeze(3).to_broadcast(by_head + [2])
+        plus_sin_heads = cos_sin[:, PAIRS:].unsqueeze(1).to_broadcast(by_head)
+        minus_sin_heads = minus_sin[:].unsqueeze(1).to_broadcast(by_head)
+
+        acc = [acc_pool.tile([P, BANK], F32, name="acc%d" % bank) for bank in range(BANKS)]
+
+        def mx_pass(bank, group, w_codes):
+            tokens = slice(group * TOKENS, (group + 1) * TOKENS)
+            nc.tensor.matmul_mx(
+                out=acc[bank][:],
+                lhsT=x_codes[:, tokens].bitcast(FP8X4),
+                lhsT_scale=x_scales[:, tokens],
+                rhs=w_codes.bitcast(FP8X4),
+                rhs_scale=w_planes[
+                    4 * (group % PLANES_PER_TILE) : P,
+                    group // PLANES_PER_TILE,
+                    bank * BANK : (bank + 1) * BANK,
+                ],
+                start=(group == 0),
+                stop=(group == GROUPS - 1),
+            )
+
+        def rotate_and_store(bank):
+            cols = slice(bank * BANK, (bank + 1) * BANK)
+            z = stage.tile([P, HEADS_PER_BANK, PAIRS, 2], F32)
+            nc.vector.tensor_add(
+                out=z[:].rearrange("p h i e -> p (h i e)"), in0=acc[bank][:], in1=bias_all[:, cols]
+            )
+            straight = stage.tile([P, HEADS_PER_BANK, PAIRS, 2], F32)
+            nc.vector.tensor_mul(out=straight[:], in0=z[:], in1=cos_pairs)
+            crossed = stage.tile([P, 2, HEADS_PER_BANK, PAIRS], F32)
+            nc.vector.tensor_mul(out=crossed[:, 0, :, :], in0=z[:, :, :, 1], in1=minus_sin_heads)
+            nc.vector.tensor_mul(out=crossed[:, 1, :, :], in0=z[:, :, :, 0], in1=plus_sin_heads)
+            turned_z = stage.tile([P, HEADS_PER_BANK, PAIRS, 2], F32)
+            nc.vector.tensor_add(
+                out=turned_z[:], in0=straight[:], in1=crossed[:].rearrange("p e h i -> p h i e")
+            )
+            heads = slice(bank * HEADS_PER_BANK, (bank + 1) * HEADS_PER_BANK)
+            nc.sync.dma_start(
+                out=out[0, heads, :, :].rearrange("h m j -> m h j"),
+                in_=turned_z[:].rearrange("p h i e -> p h (i e)"),
+            )
+
+        bank_bytes = BANK * PACK
+        for step in range(W_STEPS):
+            if step + W_AHEAD < W_STEPS:
+                w_tiles.append(load_weights(step + W_AHEAD))
+            w_tile = w_tiles[step]
+            if step < WHOLE_GROUPS:
+                for bank in range(BANKS):
+                    mx_pass(bank, step, w_tile[:, bank * bank_bytes : (bank + 1) * bank_bytes])
+            else:
+                bank = step - WHOLE_GROUPS
+                for late in range(BANKS):
+                    mx_pass(
+                        bank, WHOLE_GROUPS + late, w_tile[:, late * bank_bytes : (late + 1) * bank_bytes]
+                    )
+                rotate_and_store(bank)

@@ -34,11 +34,23 @@ GROUPS_PER_BANK = 2
 PLANES_PER_TILE = 4
 PLANE_TILES = GROUPS // PLANES_PER_TILE
 
-WHOLE_GROUPS = GROUPS - BANKS
-W_STEPS = WHOLE_GROUPS + BANKS
+LATE_GROUPS = 8
+WHOLE_GROUPS = GROUPS - LATE_GROUPS
+LATE_WIDTHS = (512, 512, 512, 256, 128, 128)
+LATE_STARTS = tuple(sum(LATE_WIDTHS[:n]) for n in range(len(LATE_WIDTHS)))
+LATE_LOAD = 1024
+LATE_LOAD_GROUPS = tuple(min(LATE_GROUPS // 2, LATE_LOAD // width) for width in LATE_WIDTHS)
+
+LOADS = [(group, 1, 0, D) for group in range(WHOLE_GROUPS)] + [
+    (group, groups, start_col, width)
+    for groups, start_col, width in zip(LATE_LOAD_GROUPS, LATE_STARTS, LATE_WIDTHS)
+    for group in range(WHOLE_GROUPS, GROUPS, groups)
+]
 W_BYTES = D * PACK
 W_BUFS = 12
 W_AHEAD = W_BUFS - 1
+
+EARLY_GROUPS = 16
 
 PI_HIGH = 3.140625
 PI_MIDDLE = int((math.pi - PI_HIGH) * 2.0**27) / 2.0**27
@@ -93,20 +105,16 @@ def tile_multiheadedattention_pa_k_kernel(tc, x, w_words, w_scales, b, out):
                 )
 
         def load_weights(step):
+            group, groups, first_col, width = LOADS[step]
             w_tile = w_pool.tile([P, W_BYTES], U8, name="w_tile", align_bytes=64)
-            if step < WHOLE_GROUPS:
-                nc.sync.dma_start(
-                    out=w_tile[:].bitcast(I32),
-                    in_=w_words[step].rearrange("p n t -> p (n t)").bitcast(I32),
-                )
-            else:
-                bank = step - WHOLE_GROUPS
-                nc.sync.dma_start(
-                    out=w_tile[:].rearrange("p (g c) -> p g c", g=BANKS).bitcast(I32),
-                    in_=w_words[WHOLE_GROUPS:, :, bank * BANK : (bank + 1) * BANK, :]
-                    .rearrange("g p n t -> p g (n t)")
-                    .bitcast(I32),
-                )
+            nc.sync.dma_start(
+                out=w_tile[:, : groups * width * PACK]
+                .rearrange("p (g c) -> p g c", g=groups)
+                .bitcast(I32),
+                in_=w_words[group : group + groups, :, first_col : first_col + width, :]
+                .rearrange("g p n t -> p g (n t)")
+                .bitcast(I32),
+            )
             return w_tile
 
         w_tiles = [load_weights(step) for step in range(W_AHEAD)]
@@ -188,66 +196,129 @@ def tile_multiheadedattention_pa_k_kernel(tc, x, w_words, w_scales, b, out):
         )
         cos_sin = keep.tile([P, 2 * PAIRS], F32)
         nc.vector.tensor_mul(out=cos_sin[:], in0=sine[:], in1=sign[:])
-        minus_sin = keep.tile([P, PAIRS], F32)
+        signed_sin = keep.tile([P, PAIRS, 2], F32)
         nc.vector.tensor_scalar(
-            out=minus_sin[:], in0=cos_sin[:, PAIRS:], scalar1=-1.0, scalar2=None, op0=ALU.mult
+            out=signed_sin[:, :, 0], in0=cos_sin[:, PAIRS:], scalar1=-1.0, scalar2=None, op0=ALU.mult
         )
-        by_head = [P, HEADS_PER_BANK, PAIRS]
-        cos_pairs = cos_sin[:, 0:PAIRS].unsqueeze(1).unsqueeze(3).to_broadcast(by_head + [2])
-        plus_sin_heads = cos_sin[:, PAIRS:].unsqueeze(1).to_broadcast(by_head)
-        minus_sin_heads = minus_sin[:].unsqueeze(1).to_broadcast(by_head)
+        nc.vector.tensor_copy(out=signed_sin[:, :, 1], in_=cos_sin[:, PAIRS:])
 
-        acc = [acc_pool.tile([P, BANK], F32, name="acc%d" % bank) for bank in range(BANKS)]
+        def tables(heads):
+            shape = [P, heads, PAIRS, 2]
+            return (
+                cos_sin[:, 0:PAIRS].unsqueeze(1).unsqueeze(3).to_broadcast(shape),
+                signed_sin[:].unsqueeze(1).to_broadcast(shape),
+            )
 
-        def mx_pass(bank, group, w_codes):
+        def bank_tile(bank):
+            return acc_pool.tile([P, BANK], F32, name="acc%d" % bank)
+
+        early = [bank_tile(bank) for bank in range(BANKS)]
+
+        base = keep.tile([P, D], F32)
+        result = keep.tile([P, D], F32)
+
+        def mx_pass(out_cols, group, first_col, width, w_codes, start, stop):
             tokens = slice(group * TOKENS, (group + 1) * TOKENS)
             nc.tensor.matmul_mx(
-                out=acc[bank][:],
+                out=out_cols,
                 lhsT=x_codes[:, tokens].bitcast(FP8X4),
                 lhsT_scale=x_scales[:, tokens],
                 rhs=w_codes.bitcast(FP8X4),
                 rhs_scale=w_planes[
                     4 * (group % PLANES_PER_TILE) : P,
                     group // PLANES_PER_TILE,
-                    bank * BANK : (bank + 1) * BANK,
+                    first_col : first_col + width,
                 ],
-                start=(group == 0),
-                stop=(group == GROUPS - 1),
+                start=start,
+                stop=stop,
             )
 
-        def rotate_and_store(bank):
-            cols = slice(bank * BANK, (bank + 1) * BANK)
-            z = stage.tile([P, HEADS_PER_BANK, PAIRS, 2], F32)
-            nc.vector.tensor_add(
-                out=z[:].rearrange("p h i e -> p (h i e)"), in0=acc[bank][:], in1=bias_all[:, cols]
+        def by_pair(ap):
+            return ap.rearrange("p (h i e) -> p h i e", i=PAIRS, e=2)
+
+        def rotate_early():
+            cos_heads, sin_heads = tables(HEADS_PER_BANK)
+            z = keep.tile([P, BANKS, BANK], F32)
+            for bank in range(BANKS):
+                cols = slice(bank * BANK, (bank + 1) * BANK)
+                nc.vector.tensor_add(out=z[:, bank, :], in0=early[bank][:], in1=bias_all[:, cols])
+            for bank in range(BANKS):
+                cols = slice(bank * BANK, (bank + 1) * BANK)
+                crossed = stage.tile([P, BANK], F32, name="crossed")
+                nc.vector.tensor_mul(
+                    out=by_pair(crossed[:]), in0=by_pair(z[:, bank, :])[:, :, :, ::-1], in1=sin_heads
+                )
+                straight = stage.tile([P, BANK], F32, name="straight")
+                nc.vector.tensor_mul(
+                    out=by_pair(straight[:]), in0=by_pair(z[:, bank, :]), in1=cos_heads
+                )
+                nc.vector.tensor_add(out=base[:, cols], in0=straight[:], in1=crossed[:])
+
+        def rotate_late(late, first_col, width):
+            heads = width // HEAD_DIM
+            cos_heads, sin_heads = tables(heads)
+            straight = stage.tile([P, BANK], F32, name="straight")
+            nc.vector.tensor_mul(out=by_pair(straight[:, :width]), in0=by_pair(late), in1=cos_heads)
+            crossed = stage.tile([P, BANK], F32, name="crossed")
+            nc.vector.tensor_mul(
+                out=by_pair(crossed[:, :width]), in0=by_pair(late)[:, :, :, ::-1], in1=sin_heads
             )
-            straight = stage.tile([P, HEADS_PER_BANK, PAIRS, 2], F32)
-            nc.vector.tensor_mul(out=straight[:], in0=z[:], in1=cos_pairs)
-            crossed = stage.tile([P, 2, HEADS_PER_BANK, PAIRS], F32)
-            nc.vector.tensor_mul(out=crossed[:, 0, :, :], in0=z[:, :, :, 1], in1=minus_sin_heads)
-            nc.vector.tensor_mul(out=crossed[:, 1, :, :], in0=z[:, :, :, 0], in1=plus_sin_heads)
-            turned_z = stage.tile([P, HEADS_PER_BANK, PAIRS, 2], F32)
             nc.vector.tensor_add(
-                out=turned_z[:], in0=straight[:], in1=crossed[:].rearrange("p e h i -> p h i e")
+                out=straight[:, :width],
+                in0=straight[:, :width],
+                in1=base[:, first_col : first_col + width],
             )
-            heads = slice(bank * HEADS_PER_BANK, (bank + 1) * HEADS_PER_BANK)
+            cols = slice(first_col, first_col + width)
+            nc.vector.tensor_add(
+                out=result[:, cols], in0=straight[:, :width], in1=crossed[:, :width]
+            )
+            first_head = first_col // HEAD_DIM
             nc.sync.dma_start(
-                out=out[0, heads, :, :].rearrange("h m j -> m h j"),
-                in_=turned_z[:].rearrange("p h i e -> p h (i e)"),
+                out=out[0, first_head : first_head + heads, :, :].rearrange("h m j -> m h j"),
+                in_=result[:, cols].rearrange("p (h j) -> p h j", h=heads),
             )
 
-        bank_bytes = BANK * PACK
-        for step in range(W_STEPS):
-            if step + W_AHEAD < W_STEPS:
+        late_sums = []
+
+        def open_late_sums():
+            for n in range(len(LATE_WIDTHS)):
+                if n < 8 - BANKS:
+                    late_sums.append(work_pool.tile([P, BANK], F32, name="work"))
+                else:
+                    late_sums.append(bank_tile(n - (8 - BANKS)))
+
+        def byte_range(first_col, width):
+            return slice(first_col * PACK, (first_col + width) * PACK)
+
+        for step, (first_group, groups, first_col, width) in enumerate(LOADS):
+            if step + W_AHEAD < len(LOADS):
                 w_tiles.append(load_weights(step + W_AHEAD))
             w_tile = w_tiles[step]
-            if step < WHOLE_GROUPS:
+            if first_group < EARLY_GROUPS:
                 for bank in range(BANKS):
-                    mx_pass(bank, step, w_tile[:, bank * bank_bytes : (bank + 1) * bank_bytes])
-            else:
-                bank = step - WHOLE_GROUPS
-                for late in range(BANKS):
                     mx_pass(
-                        bank, WHOLE_GROUPS + late, w_tile[:, late * bank_bytes : (late + 1) * bank_bytes]
+                        early[bank][:], first_group, bank * BANK, BANK,
+                        w_tile[:, byte_range(bank * BANK, BANK)],
+                        first_group == 0, first_group == EARLY_GROUPS - 1,
                     )
-                rotate_and_store(bank)
+                if first_group == EARLY_GROUPS - 1:
+                    rotate_early()
+                    open_late_sums()
+            elif first_group < WHOLE_GROUPS:
+                for n, late_width in enumerate(LATE_WIDTHS):
+                    mx_pass(
+                        late_sums[n][:, :late_width], first_group, LATE_STARTS[n], late_width,
+                        w_tile[:, byte_range(LATE_STARTS[n], late_width)],
+                        first_group == EARLY_GROUPS, False,
+                    )
+            else:
+                late_sum = late_sums[LATE_STARTS.index(first_col)][:, :width]
+                for local in range(groups):
+                    group = first_group + local
+                    mx_pass(
+                        late_sum, group, first_col, width,
+                        w_tile[:, byte_range(local * width, width)],
+                        False, group == GROUPS - 1,
+                    )
+                if first_group + groups == GROUPS:
+                    rotate_late(late_sum, first_col, width)

@@ -36,16 +36,15 @@ PLANE_TILES = GROUPS // PLANES_PER_TILE
 
 LATE_GROUPS = 8
 WHOLE_GROUPS = GROUPS - LATE_GROUPS
-LATE_WIDTHS = (512, 512, 512, 256, 128, 128)
-LATE_STARTS = tuple(sum(LATE_WIDTHS[:n]) for n in range(len(LATE_WIDTHS)))
-LATE_LOAD = 1024
-LATE_LOAD_GROUPS = tuple(min(LATE_GROUPS // 2, LATE_LOAD // width) for width in LATE_WIDTHS)
+HALF_GROUPS = WHOLE_GROUPS + LATE_GROUPS // 2
 
-LOADS = [(group, 1, 0, D) for group in range(WHOLE_GROUPS)] + [
-    (group, groups, start_col, width)
-    for groups, start_col, width in zip(LATE_LOAD_GROUPS, LATE_STARTS, LATE_WIDTHS)
-    for group in range(WHOLE_GROUPS, GROUPS, groups)
-]
+LOADS = (
+    [(group, 1, 0, 2048) for group in range(WHOLE_GROUPS)]
+    + [(group, 2, 0, 1024) for group in range(WHOLE_GROUPS, GROUPS, 2)]
+    + [(group, 4, 1024, 512) for group in range(WHOLE_GROUPS, GROUPS, 4)]
+    + [(WHOLE_GROUPS, 4, 1536, 512), (HALF_GROUPS, 4, 1536, 256), (HALF_GROUPS, 4, 1792, 256)]
+)
+LATE_RANGES = ((0, 512), (512, 512), (1024, 512), (1536, 256), (1792, 256))
 W_BYTES = D * PACK
 W_BUFS = 12
 W_AHEAD = W_BUFS - 1
@@ -281,7 +280,7 @@ def tile_multiheadedattention_pa_k_kernel(tc, x, w_words, w_scales, b, out):
         late_sums = []
 
         def open_late_sums():
-            for n in range(len(LATE_WIDTHS)):
+            for n in range(len(LATE_RANGES)):
                 if n < 8 - BANKS:
                     late_sums.append(work_pool.tile([P, BANK], F32, name="work"))
                 else:
@@ -293,32 +292,26 @@ def tile_multiheadedattention_pa_k_kernel(tc, x, w_words, w_scales, b, out):
         for step, (first_group, groups, first_col, width) in enumerate(LOADS):
             if step + W_AHEAD < len(LOADS):
                 w_tiles.append(load_weights(step + W_AHEAD))
-            w_tile = w_tiles[step]
-            if first_group < EARLY_GROUPS:
-                for bank in range(BANKS):
-                    mx_pass(
-                        early[bank][:], first_group, bank * BANK, BANK,
-                        w_tile[:, byte_range(bank * BANK, BANK)],
-                        first_group == 0, first_group == EARLY_GROUPS - 1,
-                    )
-                if first_group == EARLY_GROUPS - 1:
-                    rotate_early()
-                    open_late_sums()
-            elif first_group < WHOLE_GROUPS:
-                for n, late_width in enumerate(LATE_WIDTHS):
-                    mx_pass(
-                        late_sums[n][:, :late_width], first_group, LATE_STARTS[n], late_width,
-                        w_tile[:, byte_range(LATE_STARTS[n], late_width)],
-                        first_group == EARLY_GROUPS, False,
-                    )
-            else:
-                late_sum = late_sums[LATE_STARTS.index(first_col)][:, :width]
-                for local in range(groups):
-                    group = first_group + local
-                    mx_pass(
-                        late_sum, group, first_col, width,
-                        w_tile[:, byte_range(local * width, width)],
-                        False, group == GROUPS - 1,
-                    )
-                if first_group + groups == GROUPS:
-                    rotate_late(late_sum, first_col, width)
+            for local in range(groups):
+                group = first_group + local
+                codes = w_tiles[step][:, byte_range(local * width, width)]
+                if group < EARLY_GROUPS:
+                    for bank in range(BANKS):
+                        mx_pass(
+                            early[bank][:], group, bank * BANK, BANK,
+                            codes[:, byte_range(bank * BANK, BANK)],
+                            group == 0, group == EARLY_GROUPS - 1,
+                        )
+                    if group == EARLY_GROUPS - 1:
+                        rotate_early()
+                        open_late_sums()
+                    continue
+                for late_sum, (late_col, late_width) in zip(late_sums, LATE_RANGES):
+                    if first_col <= late_col < first_col + width:
+                        mx_pass(
+                            late_sum[:, :late_width], group, late_col, late_width,
+                            codes[:, byte_range(late_col - first_col, late_width)],
+                            group == EARLY_GROUPS, group == GROUPS - 1,
+                        )
+                        if group == GROUPS - 1:
+                            rotate_late(late_sum[:, :late_width], late_col, late_width)

@@ -92,16 +92,22 @@ def tile_multiheadedattention_pa_k_kernel(tc, x, w_words, w_scales, b, out):
             nc.sync.dma_start(out=x_tile[:], in_=x[0, :, load * x_cols : (load + 1) * x_cols])
             x_raw.append(x_tile)
 
+        def load_planes(engine, dtype, j, quadrant):
+            engine.dma_start(
+                out=w_planes[32 * quadrant : 32 * quadrant + 16, j, :].bitcast(dtype),
+                in_=w_scales[
+                    PLANES_PER_TILE * j : PLANES_PER_TILE * (j + 1),
+                    4 * quadrant : 4 * quadrant + 4,
+                    :,
+                ].bitcast(dtype),
+            )
+
+        gate = keep.tile([P, 2], BF16)
+        nc.gpsimd.tensor_copy(out=gate[:], in_=x_raw[X_LOADS - 2][:, 0:2])
         for j in range(PLANE_TILES):
-            for quadrant in (0, 2, 1, 3):
-                nc.sync.dma_start(
-                    out=w_planes[32 * quadrant : 32 * quadrant + 16, j, :].bitcast(I32),
-                    in_=w_scales[
-                        PLANES_PER_TILE * j : PLANES_PER_TILE * (j + 1),
-                        4 * quadrant : 4 * quadrant + 4,
-                        :,
-                    ].bitcast(I32),
-                )
+            load_planes(nc.gpsimd, F32, j, 2)
+            for quadrant in (0, 3, 1):
+                load_planes(nc.sync, I32, j, quadrant)
 
         def load_weights(step):
             group, groups, first_col, width = LOADS[step]

@@ -42,7 +42,8 @@ LOADS = (
     [(group, 1, 0, 2048) for group in range(WHOLE_GROUPS)]
     + [(group, 2, 0, 1024) for group in range(WHOLE_GROUPS, GROUPS, 2)]
     + [(group, 4, 1024, 512) for group in range(WHOLE_GROUPS, GROUPS, 4)]
-    + [(WHOLE_GROUPS, 4, 1536, 512), (HALF_GROUPS, 4, 1536, 256), (HALF_GROUPS, 4, 1792, 256)]
+    + [(WHOLE_GROUPS, 4, 1536, 512)]
+    + [(group, 2, col, 256) for col in (1536, 1792) for group in range(HALF_GROUPS, GROUPS, 2)]
 )
 LATE_RANGES = ((0, 512), (512, 512), (1024, 512), (1536, 256), (1792, 256))
 W_BYTES = D * PACK
@@ -260,28 +261,33 @@ def tile_multiheadedattention_pa_k_kernel(tc, x, w_words, w_scales, b, out):
                 nc.vector.tensor_add(out=base[:, cols], in0=straight[:], in1=crossed[:])
 
         def rotate_late(late, first_col, width):
-            heads = width // HEAD_DIM
+            half = width // 2
+            heads = half // HEAD_DIM
             cos_heads, sin_heads = tables(heads)
             straight = stage.tile([P, BANK], F32, name="straight")
-            nc.vector.tensor_mul(out=by_pair(straight[:, :width]), in0=by_pair(late), in1=cos_heads)
             crossed = stage.tile([P, BANK], F32, name="crossed")
-            nc.vector.tensor_mul(
-                out=by_pair(crossed[:, :width]), in0=by_pair(late)[:, :, :, ::-1], in1=sin_heads
-            )
-            nc.vector.tensor_add(
-                out=straight[:, :width],
-                in0=straight[:, :width],
-                in1=base[:, first_col : first_col + width],
-            )
-            cols = slice(first_col, first_col + width)
-            nc.vector.tensor_add(
-                out=result[:, cols], in0=straight[:, :width], in1=crossed[:, :width]
-            )
-            first_head = first_col // HEAD_DIM
-            nc.sync.dma_start(
-                out=out[0, first_head : first_head + heads, :, :].rearrange("h m j -> m h j"),
-                in_=result[:, cols].rearrange("p (h j) -> p h j", h=heads),
-            )
+            halves = [slice(0, half), slice(half, width)]
+            for cols in halves:
+                pairs = by_pair(late[:, cols])
+                nc.vector.tensor_mul(out=by_pair(straight[:, cols]), in0=pairs, in1=cos_heads)
+                nc.vector.tensor_mul(
+                    out=by_pair(crossed[:, cols]), in0=pairs[:, :, :, ::-1], in1=sin_heads
+                )
+            for cols in halves:
+                nc.vector.tensor_add(
+                    out=straight[:, cols],
+                    in0=straight[:, cols],
+                    in1=base[:, first_col + cols.start : first_col + cols.stop],
+                )
+            for cols in halves:
+                col = first_col + cols.start
+                turned_cols = result[:, col : col + half]
+                nc.vector.tensor_add(out=turned_cols, in0=straight[:, cols], in1=crossed[:, cols])
+                head = col // HEAD_DIM
+                nc.sync.dma_start(
+                    out=out[0, head : head + heads, :, :].rearrange("h m j -> m h j"),
+                    in_=turned_cols.rearrange("p (h j) -> p h j", h=heads),
+                )
 
         late_sums = []
 

@@ -93,22 +93,24 @@ def tile_multiheadedattention_pa_k_kernel(tc, x, w_words, w_scales, b, out):
             nc.sync.dma_start(out=x_tile[:], in_=x[0, :, load * x_cols : (load + 1) * x_cols])
             x_raw.append(x_tile)
 
-        def load_planes(engine, dtype, j, quadrant):
-            engine.dma_start(
-                out=w_planes[32 * quadrant : 32 * quadrant + 16, j, :].bitcast(dtype),
-                in_=w_scales[
-                    PLANES_PER_TILE * j : PLANES_PER_TILE * (j + 1),
-                    4 * quadrant : 4 * quadrant + 4,
-                    :,
-                ].bitcast(dtype),
-            )
-
         gate = keep.tile([P, 2], BF16)
         nc.gpsimd.tensor_copy(out=gate[:], in_=x_raw[X_LOADS - 2][:, 0:2])
+        by_row = w_scales.rearrange("(j a) q n -> q a j n", a=PLANES_PER_TILE)
+        for row in range(4):
+            nc.gpsimd.dma_start(
+                out=w_planes[64 + row : 80 : PLANES_PER_TILE, :, :].bitcast(F32),
+                in_=by_row[8 + row].bitcast(F32),
+            )
         for j in range(PLANE_TILES):
-            load_planes(nc.gpsimd, F32, j, 2)
             for quadrant in (0, 3, 1):
-                load_planes(nc.sync, I32, j, quadrant)
+                nc.sync.dma_start(
+                    out=w_planes[32 * quadrant : 32 * quadrant + 16, j, :].bitcast(I32),
+                    in_=w_scales[
+                        PLANES_PER_TILE * j : PLANES_PER_TILE * (j + 1),
+                        4 * quadrant : 4 * quadrant + 4,
+                        :,
+                    ].bitcast(I32),
+                )
 
         def load_weights(step):
             group, groups, first_col, width = LOADS[step]

import math
from contextlib import ExitStack

import concourse.mybir as mybir
from concourse.masks import make_identity

F32 = mybir.dt.float32
BF16 = mybir.dt.bfloat16
I32 = mybir.dt.int32
U32 = mybir.dt.uint32
U8 = mybir.dt.uint8
FP8X4 = mybir.dt.float8_e4m3fn_x4
ALU = mybir.AluOpType
ACT = mybir.ActivationFunctionType

P = 128
PACK = 4
K_PASS = P * PACK
TOKENS = 128
K = 16384
D = 2048
HEADS = 16
HEAD_DIM = 128
PAIRS = HEAD_DIM // 2
GROUPS = K // K_PASS
BANK = 512
BANKS = D // BANK
HEADS_PER_BANK = BANK // HEAD_DIM

X_LOADS = 4
GROUPS_PER_LOAD = GROUPS // X_LOADS
GROUPS_PER_BANK = 2

PLANES_PER_TILE = 4
PLANE_TILES = GROUPS // PLANES_PER_TILE

LATE_GROUPS = 8
WHOLE_GROUPS = GROUPS - LATE_GROUPS
HALF_GROUPS = WHOLE_GROUPS + LATE_GROUPS // 2

LOADS = (
    [(group, 1, 0, 2048) for group in range(WHOLE_GROUPS)]
    + [(group, 2, 0, 1024) for group in range(WHOLE_GROUPS, GROUPS, 2)]
    + [(group, 4, 1024, 512) for group in range(WHOLE_GROUPS, GROUPS, 4)]
    + [(WHOLE_GROUPS, 4, 1536, 512)]
    + [(group, 2, col, 256) for col in (1536, 1792) for group in range(HALF_GROUPS, GROUPS, 2)]
)
LATE_RANGES = ((0, 512), (512, 512), (1024, 512), (1536, 256), (1792, 256))
W_BYTES = D * PACK
W_BUFS = 12
W_AHEAD = W_BUFS - 1

EARLY_GROUPS = 16

PI_HIGH = 3.140625
PI_MIDDLE = int((math.pi - PI_HIGH) * 2.0**27) / 2.0**27
PI_LOW = math.pi - PI_HIGH - PI_MIDDLE

FLOPS = 2 * TOKENS * K * D


def tile_multiheadedattention_pa_k_kernel(tc, x, w_words, w_scales, b, out):
    nc = tc.nc
    with ExitStack() as ctx:
        ctx.enter_context(tc.manual_schedule())
        keep = ctx.enter_context(tc.tile_pool(name="keep", bufs=1))
        x_pool = ctx.enter_context(tc.tile_pool(name="x_pool", bufs=X_LOADS))
        stage = ctx.enter_context(tc.tile_pool(name="stage", bufs=2))
        w_pool = ctx.enter_context(tc.tile_pool(name="w_pool", bufs=W_BUFS))
        acc_pool = ctx.enter_context(tc.psum_pool(name="acc_pool", bufs=1))
        work_pool = ctx.enter_context(tc.psum_pool(name="work_pool", bufs=8 - BANKS))

        identity = keep.tile([P, P], F32)
        make_identity(nc, identity[:])
        pair_index = keep.tile([P, PAIRS], I32)
        nc.gpsimd.iota(pair_index[:], pattern=[[1, PAIRS]], base=0, channel_multiplier=0)
        position = keep.tile([P, 1], I32)
        nc.gpsimd.iota(position[:], pattern=[[0, 1]], base=0, channel_multiplier=1)

        bias_row = keep.tile([P, D], BF16)
        nc.vector.memset(bias_row[:], 0.0)
        ones = keep.tile([P, P], BF16)
        nc.vector.memset(ones[:], 1.0)
        w_planes = keep.tile([P, PLANE_TILES, D], U8, align_bytes=64)
        nc.vector.memset(w_planes[:].bitcast(I32), 0)

        nc.scalar.dma_start(out=bias_row[0:1, :], in_=b.rearrange("(o n) -> o n", o=1))

        x_cols = K // X_LOADS
        x_raw = []
        for load in range(X_LOADS):
            x_tile = x_pool.tile([P, x_cols], BF16, name="x_tile")
            nc.sync.dma_start(out=x_tile[:], in_=x[0, :, load * x_cols : (load + 1) * x_cols])
            x_raw.append(x_tile)

        gate = keep.tile([P, 2], BF16)
        nc.gpsimd.tensor_copy(out=gate[:], in_=x_raw[X_LOADS - 2][:, 0:2])
        by_row = w_scales.rearrange("(j a) q n -> q a j n", a=PLANES_PER_TILE)
        for row in range(4):
            nc.gpsimd.dma_start(
                out=w_planes[64 + row : 80 : PLANES_PER_TILE, :, :].bitcast(F32),
                in_=by_row[8 + row].bitcast(F32),
            )
        for j in range(PLANE_TILES):
            for quadrant in (0, 3, 1):
                nc.sync.dma_start(
                    out=w_planes[32 * quadrant : 32 * quadrant + 16, j, :].bitcast(I32),
                    in_=w_scales[
                        PLANES_PER_TILE * j : PLANES_PER_TILE * (j + 1),
                        4 * quadrant : 4 * quadrant + 4,
                        :,
                    ].bitcast(I32),
                )

        def load_weights(step):
            group, groups, first_col, width = LOADS[step]
            w_tile = w_pool.tile([P, W_BYTES], U8, name="w_tile", align_bytes=64)
            nc.sync.dma_start(
                out=w_tile[:, : groups * width * PACK]
                .rearrange("p (g c) -> p g c", g=groups)
                .bitcast(I32),
                in_=w_words[group : group + groups, :, first_col : first_col + width, :]
                .rearrange("g p n t -> p g (n t)")
                .bitcast(I32),
            )
            return w_tile

        w_tiles = [load_weights(step) for step in range(W_AHEAD)]

        x_codes = keep.tile([P, GROUPS * TOKENS], U32, align_bytes=64)
        x_scales = keep.tile([P, GROUPS * TOKENS], U8, align_bytes=64)
        for load in range(X_LOADS):
            x_words = x_raw[load][:].bitcast(F32)
            grouped = stage.tile([P, GROUPS_PER_LOAD, TOKENS, PACK], BF16, align_bytes=64)
            for bank in range(GROUPS_PER_LOAD // GROUPS_PER_BANK):
                turned = work_pool.tile([P, GROUPS_PER_BANK, 2, TOKENS], F32, name="work")
                for local in range(GROUPS_PER_BANK):
                    first = (K_PASS // 2) * (bank * GROUPS_PER_BANK + local)
                    for u in range(2):
                        nc.tensor.transpose(
                            turned[:, local, u, :],
                            x_words[:, first + u : first + K_PASS // 2 : 2],
                            identity[:],
                        )
                groups = slice(bank * GROUPS_PER_BANK, (bank + 1) * GROUPS_PER_BANK)
                side_by_side = grouped[:, groups, :, :].bitcast(F32)
                if bank % 2 == 0:
                    nc.scalar.copy(out=side_by_side, in_=turned[:].rearrange("p g u m -> p g m u"))
                else:
                    nc.vector.tensor_copy(
                        out=side_by_side, in_=turned[:].rearrange("p g u m -> p g m u")
                    )
            cols = slice(load * GROUPS_PER_LOAD * TOKENS, (load + 1) * GROUPS_PER_LOAD * TOKENS)
            nc.vector.quantize_mx(
                out=x_codes[:, cols].bitcast(FP8X4),
                scales=x_scales[:, cols],
                in_=grouped[:].rearrange("p g m t -> p (g m t)"),
            )

        bias_all = keep.tile([P, D], F32)
        for bank in range(BANKS):
            cols = slice(bank * BANK, (bank + 1) * BANK)
            spread = work_pool.tile([P, BANK], F32, name="work")
            nc.tensor.matmul(out=spread[:], lhsT=ones[:], rhs=bias_row[:, cols], start=True, stop=True)
            nc.scalar.copy(out=bias_all[:, cols], in_=spread[:])

        pair_f = keep.tile([P, PAIRS], F32)
        nc.vector.tensor_copy(out=pair_f[:], in_=pair_index[:])
        position_f = keep.tile([P, 1], F32)
        nc.vector.tensor_copy(out=position_f[:], in_=position[:])
        frequency = keep.tile([P, PAIRS], F32)
        nc.scalar.activation(
            out=frequency[:], in_=pair_f[:], func=ACT.Exp, scale=-2.0 * math.log(10000.0) / HEAD_DIM
        )
        angle = keep.tile([P, 2 * PAIRS], F32)
        nc.vector.tensor_scalar(
            out=angle[:, 0:PAIRS], in0=frequency[:], scalar1=position_f[:, 0:1],
            scalar2=math.pi / 2.0, op0=ALU.mult, op1=ALU.add,
        )
        nc.vector.tensor_scalar(
            out=angle[:, PAIRS:], in0=frequency[:], scalar1=position_f[:, 0:1],
            scalar2=None, op0=ALU.mult,
        )
        half_turns_f = keep.tile([P, 2 * PAIRS], F32)
        nc.vector.tensor_scalar(
            out=half_turns_f[:], in0=angle[:], scalar1=1.0 / math.pi, scalar2=None, op0=ALU.mult
        )
        half_turns_i = keep.tile([P, 2 * PAIRS], I32)
        nc.vector.tensor_copy(out=half_turns_i[:], in_=half_turns_f[:])
        half_turns = keep.tile([P, 2 * PAIRS], F32)
        nc.vector.tensor_copy(out=half_turns[:], in_=half_turns_i[:])
        for part in (PI_HIGH, PI_MIDDLE, PI_LOW):
            nc.vector.scalar_tensor_tensor(
                out=angle[:], in0=half_turns[:], scalar=-part, in1=angle[:],
                op0=ALU.mult, op1=ALU.add,
            )
        sine = keep.tile([P, 2 * PAIRS], F32)
        nc.scalar.activation(out=sine[:], in_=angle[:], func=ACT.Sin)
        odd = keep.tile([P, 2 * PAIRS], I32)
        nc.vector.tensor_single_scalar(out=odd[:], in_=half_turns_i[:], scalar=1, op=ALU.bitwise_and)
        sign = keep.tile([P, 2 * PAIRS], F32)
        nc.vector.tensor_scalar(
            out=sign[:], in0=odd[:], scalar1=-2.0, scalar2=1.0, op0=ALU.mult, op1=ALU.add
        )
        cos_sin = keep.tile([P, 2 * PAIRS], F32)
        nc.vector.tensor_mul(out=cos_sin[:], in0=sine[:], in1=sign[:])
        signed_sin = keep.tile([P, PAIRS, 2], F32)
        nc.vector.tensor_scalar(
            out=signed_sin[:, :, 0], in0=cos_sin[:, PAIRS:], scalar1=-1.0, scalar2=None, op0=ALU.mult
        )
        nc.vector.tensor_copy(out=signed_sin[:, :, 1], in_=cos_sin[:, PAIRS:])

        def tables(heads):
            shape = [P, heads, PAIRS, 2]
            return (
                cos_sin[:, 0:PAIRS].unsqueeze(1).unsqueeze(3).to_broadcast(shape),
                signed_sin[:].unsqueeze(1).to_broadcast(shape),
            )

        def bank_tile(bank):
            return acc_pool.tile([P, BANK], F32, name="acc%d" % bank)

        early = [bank_tile(bank) for bank in range(BANKS)]

        base = keep.tile([P, D], F32)
        result = keep.tile([P, D], F32)

        def mx_pass(out_cols, group, first_col, width, w_codes, start, stop):
            tokens = slice(group * TOKENS, (group + 1) * TOKENS)
            nc.tensor.matmul_mx(
                out=out_cols,
                lhsT=x_codes[:, tokens].bitcast(FP8X4),
                lhsT_scale=x_scales[:, tokens],
                rhs=w_codes.bitcast(FP8X4),
                rhs_scale=w_planes[
                    4 * (group % PLANES_PER_TILE) : P,
                    group // PLANES_PER_TILE,
                    first_col : first_col + width,
                ],
                start=start,
                stop=stop,
            )

        def by_pair(ap):
            return ap.rearrange("p (h i e) -> p h i e", i=PAIRS, e=2)

        def rotate_early():
            cos_heads, sin_heads = tables(HEADS_PER_BANK)
            z = keep.tile([P, BANKS, BANK], F32)
            for bank in range(BANKS):
                cols = slice(bank * BANK, (bank + 1) * BANK)
                nc.vector.tensor_add(out=z[:, bank, :], in0=early[bank][:], in1=bias_all[:, cols])
            for bank in range(BANKS):
                cols = slice(bank * BANK, (bank + 1) * BANK)
                crossed = stage.tile([P, BANK], F32, name="crossed")
                nc.vector.tensor_mul(
                    out=by_pair(crossed[:]), in0=by_pair(z[:, bank, :])[:, :, :, ::-1], in1=sin_heads
                )
                straight = stage.tile([P, BANK], F32, name="straight")
                nc.vector.tensor_mul(
                    out=by_pair(straight[:]), in0=by_pair(z[:, bank, :]), in1=cos_heads
                )
                nc.vector.tensor_add(out=base[:, cols], in0=straight[:], in1=crossed[:])

        def rotate_late(late, first_col, width):
            half = width // 2
            heads = half // HEAD_DIM
            cos_heads, sin_heads = tables(heads)
            straight = stage.tile([P, BANK], F32, name="straight")
            crossed = stage.tile([P, BANK], F32, name="crossed")
            halves = [slice(0, half), slice(half, width)]
            for cols in halves:
                pairs = by_pair(late[:, cols])
                nc.vector.tensor_mul(out=by_pair(straight[:, cols]), in0=pairs, in1=cos_heads)
                nc.vector.tensor_mul(
                    out=by_pair(crossed[:, cols]), in0=pairs[:, :, :, ::-1], in1=sin_heads
                )
            for cols in halves:
                nc.vector.tensor_add(
                    out=straight[:, cols],
                    in0=straight[:, cols],
                    in1=base[:, first_col + cols.start : first_col + cols.stop],
                )
            for cols in halves:
                col = first_col + cols.start
                turned_cols = result[:, col : col + half]
                nc.vector.tensor_add(out=turned_cols, in0=straight[:, cols], in1=crossed[:, cols])
                head = col // HEAD_DIM
                nc.sync.dma_start(
                    out=out[0, head : head + heads, :, :].rearrange("h m j -> m h j"),
                    in_=turned_cols.rearrange("p (h j) -> p h j", h=heads),
                )

        late_sums = []

        def open_late_sums():
            for n in range(len(LATE_RANGES)):
                if n < 8 - BANKS:
                    late_sums.append(work_pool.tile([P, BANK], F32, name="work"))
                else:
                    late_sums.append(bank_tile(n - (8 - BANKS)))

        def byte_range(first_col, width):
            return slice(first_col * PACK, (first_col + width) * PACK)

        for step, (first_group, groups, first_col, width) in enumerate(LOADS):
            if step + W_AHEAD < len(LOADS):
                w_tiles.append(load_weights(step + W_AHEAD))
            for local in range(groups):
                group = first_group + local
                codes = w_tiles[step][:, byte_range(local * width, width)]
                if group < EARLY_GROUPS:
                    for bank in range(BANKS):
                        mx_pass(
                            early[bank][:], group, bank * BANK, BANK,
                            codes[:, byte_range(bank * BANK, BANK)],
                            group == 0, group == EARLY_GROUPS - 1,
                        )
                    if group == EARLY_GROUPS - 1:
                        rotate_early()
                        open_late_sums()
                    continue
                for late_sum, (late_col, late_width) in zip(late_sums, LATE_RANGES):
                    if first_col <= late_col < first_col + width:
                        mx_pass(
                            late_sum[:, :late_width], group, late_col, late_width,
                            codes[:, byte_range(late_col - first_col, late_width)],
                            group == EARLY_GROUPS, group == GROUPS - 1,
                        )
                        if group == GROUPS - 1:
                            rotate_late(late_sum[:, :late_width], late_col, late_width)
